import numpy as np
import ml_dtypes


def mxq(x, axis, fmt="e4m3"):
    dtype, down = {"e4m3": (ml_dtypes.float8_e4m3fn, 7), "e5m2": (ml_dtypes.float8_e5m2, 14)}[fmt]
    v = np.moveaxis(np.asarray(x, np.float32).astype(ml_dtypes.bfloat16).astype(np.float64), axis, -1)
    blocks = v.reshape(v.shape[:-1] + (-1, 32))
    amax = np.abs(blocks).max(-1, keepdims=True)
    byte = np.maximum(np.where(amax > 0, np.frexp(amax)[1] - 1 + 127, 0) - down, 1)
    scale = np.exp2(byte - 127.0)
    codes = (blocks / scale).astype(np.float32).astype(dtype).astype(np.float64)
    return np.moveaxis((codes * scale).reshape(v.shape), -1, axis)


WIDE = False


def mx_kscale(k):
    if not WIDE:
        return np.ones(k)
    levels = np.array([10, -10, 5, -5, 0])
    if k % 512:
        return np.exp2(np.random.permutation(np.resize(levels, k // 32))).repeat(32)
    a = np.empty((k // 512, 16))
    for p in range(k // 512):
        a[p, :8] = np.random.permutation(np.resize(levels, 8))
        for g in range(8):
            far = levels[np.abs(levels - a[p, g]) >= 10]
            a[p, g + 8] = far[np.random.randint(len(far))]
    return np.exp2(a.ravel()).repeat(32)


BF16 = ml_dtypes.bfloat16


def bf(x):
    return np.asarray(x, np.float32).astype(BF16)


def f64(x):
    return np.asarray(x).astype(np.float64)


N, N_CH, X, H = 512, 5, 512, 512
K = N_CH * H


def sigmoid(v):
    return 1.0 / (1.0 + np.exp(-v))


def setup_inputs():
    s, t = mx_kscale(X), mx_kscale(K)
    return {
        "x": bf(np.random.standard_normal((N, X)) * s),
        "x_mask": bf(np.random.random(N) < 0.75),
        "neighbour_h": bf(np.random.standard_normal((N, N_CH, H)) * t.reshape(N_CH, H)),
        "neighbour_c": bf(np.random.standard_normal((N, N_CH, H))),
        "W_f_in": bf(np.random.standard_normal((X, H)) * 0.5 / np.sqrt(X) / s[:, None]),
        "b_f_in": bf(np.random.standard_normal(H) * 0.3),
        "W_aggr_f": bf(np.random.standard_normal((K, K)) / np.sqrt(K) / t[:, None]),
        "b_aggr_f": bf(np.random.standard_normal(K) * 0.3),
    }


def core(x, x_mask, neighbour_h, neighbour_c, W_f_in, b_f_in, W_aggr_f, b_aggr_f):
    h_flat = f64(neighbour_h).reshape(N, K)
    f_input = ((mxq(f64(x), 1, "e4m3") @ mxq(f64(W_f_in), 0, "e4m3")) + f64(b_f_in)) * f64(x_mask)[:, None]
    f_input = np.tile(f_input, (1, N_CH))
    f_gate = (mxq(h_flat, 1, "e4m3") @ mxq(f64(W_aggr_f), 0, "e4m3")) + f64(b_aggr_f) + f_input
    f_aggr = f_gate + f_input
    f = sigmoid(f_aggr).reshape(N, N_CH, H)
    return np.sum(f * f64(neighbour_c), axis=1)


def e4m3fn_bytes(y):
    return np.clip(np.asarray(y, np.float64), -448.0, 448.0).astype(np.float32).astype(ml_dtypes.float8_e4m3fn).view(np.uint8)


Y_SCALE = 160.0


def reference(x, x_mask, neighbour_h, neighbour_c, W_f_in, b_f_in, W_aggr_f, b_aggr_f):
    out = core(x, x_mask, neighbour_h, neighbour_c, W_f_in, b_f_in, W_aggr_f, b_aggr_f)
    return out, e4m3fn_bytes(out * Y_SCALE)

@@ -1,0 +1,485 @@
+from contextlib import ExitStack
+
+import concourse.mybir as mybir
+from concourse.masks import make_identity
+
+FLOPS = 2 * 512 * 2560 * 2560 + 2 * 512 * 512 * 512
+
+F32 = mybir.dt.float32
+BF16 = mybir.dt.bfloat16
+U32 = mybir.dt.uint32
+U8 = mybir.dt.uint8
+FP8X4 = mybir.dt.float8_e4m3fn_x4
+FP8 = mybir.dt.float8_e4m3fn
+ACT = mybir.ActivationFunctionType
+ALU = mybir.AluOpType
+
+P = 128
+NODES = 512
+NT = 4
+NCH = 5
+H = 512
+JT = 4
+NG = 5
+TILES = NCH * JT
+Y_SCALE = 160.0
+V_WF = 256
+V_SHARE = (256, 160, 160, 160)
+G_SHARE = (0, 0, 0, 0)
+G_LAST = 0
+V_LAST = 48
+AHEAD = 4
+EVAC_V = (0, 2, 4, 6, 8, 10)
+MANUAL = False
+QFIRST = (2, 3, 4)
+LOOK_FROM = 5
+N_HALVED = 1
+OUT_V = (("b", 2), ("b", 3), ("b", 0), ("b", 1))
+OUT_S = (("f", 0), ("f", 1), ("f", 2), ("f", 3))
+TURN_DUMMY = 0
+HEAD_DUMMY = {0: 2, 1: 2, 2: 2, 3: 2, 4: 2}
+BOUND_DUMMY = 4
+
+
+def tile_treelstmcell_pa_kernel(
+    tc, x, x_mask, neighbour_h, neighbour_c, W_f_in, b_f_in, W_aggr_f, b_aggr_f, out_0, out_1
+):
+    nc = tc.nc
+    with ExitStack() as ctx:
+        const = ctx.enter_context(tc.tile_pool(name="const", bufs=1))
+        head = ctx.enter_context(tc.tile_pool(name="head", bufs=1))
+        wraw_pool = ctx.enter_context(tc.tile_pool(name="wraw", bufs=AHEAD + 1))
+        wg_pool = ctx.enter_context(tc.tile_pool(name="wg", bufs=3))
+        wc_pool = ctx.enter_context(tc.tile_pool(name="wc", bufs=7))
+        nc_pool = ctx.enter_context(tc.tile_pool(name="ncp", bufs=4))
+        z_pool = ctx.enter_context(tc.tile_pool(name="zp", bufs=3))
+        f_pool = ctx.enter_context(tc.tile_pool(name="fp", bufs=4))
+        pr_pool = ctx.enter_context(tc.tile_pool(name="prp", bufs=3))
+        out_pool = ctx.enter_context(tc.tile_pool(name="outp", bufs=4))
+        psum = ctx.enter_context(tc.psum_pool(name="psum", bufs=1))
+        if MANUAL:
+            ctx.enter_context(tc.manual_schedule())
+
+        warm = const.tile([P, 2], F32, name="warm")
+        nc.vector.memset(warm[:], 0.0)
+        nc.scalar.activation(out=warm[:, 1:2], in_=warm[:, 0:1], func=ACT.Sigmoid)
+
+        ident_f = const.tile([P, P], F32, name="ident_f")
+        make_identity(nc, ident_f[:])
+        brow = const.tile([P, P], BF16, name="brow")
+        nc.vector.memset(brow[:], 0.0)
+        mrow = const.tile([P, NODES], BF16, name="mrow")
+        nc.vector.memset(mrow[:], 0.0)
+        ident_b = const.tile([P, P], BF16, name="ident_b")
+        make_identity(nc, ident_b[:])
+        ones_b = const.tile([P, P], BF16, name="ones_b")
+        nc.vector.memset(ones_b[:], 1.0)
+
+        units = [(0, g, 1) for g in range(NG)]
+        units += [(c, g0, ng) for c in range(1, NCH - 1) for (g0, ng) in ((0, 2), (2, 2), (4, 1))]
+        n_chunk_units = len(units)
+        n_units = n_chunk_units + JT
+        unit_of = {}
+        for u in range(n_chunk_units):
+            for i in range(units[u][2]):
+                unit_of[(units[u][0], units[u][1] + i)] = (u, i)
+        raws = {}
+        groups = {}
+        codes = {}
+        ncs = {}
+
+        def w_chunk(c, g):
+            return W_aggr_f[512 * g:512 * (g + 1), H * c:H * (c + 1)].rearrange("(p j) w -> p j w", j=4)
+
+        def load_nc(c):
+            nct = nc_pool.tile([P, NT, H], BF16, name="nct")
+            nc.sync.dma_start(out=nct[:], in_=neighbour_c[:, c, :].rearrange("(t p) h -> p t h", p=P))
+            ncs[c] = nct
+
+        def load_unit(u):
+            if u < n_chunk_units:
+                c, g0, ng = units[u]
+                raw = wraw_pool.tile([P, 4, 2 * H], BF16, name="wraw")
+                for i in range(ng):
+                    nc.sync.dma_start(out=raw[:, :, i * H:(i + 1) * H], in_=w_chunk(c, g0 + i))
+                raws[u] = raw
+                if g0 == 4:
+                    load_nc(c)
+            elif u == n_chunk_units:
+                raw = head.tile([P, NG, 4, H], BF16, name="w4raw", tag="big", align_bytes=64)
+                for g in range(NG):
+                    nc.sync.dma_start(out=raw[:, g, :, :], in_=w_chunk(NCH - 1, g))
+                raws["last"] = raw
+                load_nc(NCH - 1)
+
+        x_sb = head.tile([P, NT, 512], BF16, name="x_sb")
+        wf_raw = head.tile([P, 4, H], BF16, name="wf_raw")
+        hf = neighbour_h.rearrange("n c h -> n (c h)")
+        nh_sb = []
+        for t in range(NT):
+            nh_t = head.tile([P, NCH * H], BF16, name="nh%d" % t)
+            nh_sb.append(nh_t)
+        for item in (0, 1, "small", "x", "wf", -1, -2, 2, -3, -4, 3, 4):
+            if item == "small":
+                nc.sync.dma_start(out=brow[0:20, :], in_=b_aggr_f.rearrange("(r p) -> r p", p=P))
+                nc.sync.dma_start(out=brow[20:24, :], in_=b_f_in.rearrange("(r p) -> r p", p=P))
+                nc.sync.dma_start(out=mrow[0:1, :], in_=x_mask.rearrange("(o n) -> o n", o=1))
+            elif item == "x":
+                nc.sync.dma_start(out=x_sb[:], in_=x.rearrange("(t p) k -> p t k", p=P))
+            elif item == "wf":
+                nc.sync.dma_start(out=wf_raw[:], in_=W_f_in.rearrange("(p j) w -> p j w", j=4))
+            elif item < 0:
+                t = -item - 1
+                nc.sync.dma_start(out=nh_sb[t][:], in_=hf[t * P:(t + 1) * P, :])
+            else:
+                load_unit(item)
+
+        hg = head.tile([P, NG + 1, NODES, 4], BF16, name="hg", tag="big", align_bytes=64)
+        hg_w = hg[:].bitcast(F32)
+        hcodes = head.tile([P, NG + 1, NODES], U32, name="hcodes", align_bytes=64)
+        hscales = head.tile([P, NG + 1, NODES], U8, name="hscales", align_bytes=64)
+        scr = psum.tile([P, NODES], F32, name="scr", tag="o3")
+        banks = [0]
+
+        def turn(g, tp):
+            b = banks[0]
+            banks[0] += 1
+            xt = psum.tile([P, 2, 2, P], F32, name="xt", tag=("t0", "t1", "a0", "a1")[b % 4])
+            for s in range(2):
+                t = 2 * tp + s
+                for u in range(2):
+                    if g < NG:
+                        src = nh_sb[t][:].bitcast(F32)[:, 256 * g + u:256 * (g + 1):2]
+                    else:
+                        src = x_sb[:, t, :].bitcast(F32)[:, u:256:2]
+                    nc.tensor.transpose(xt[:, s, u, :], src, ident_f[:])
+            for r in range(TURN_DUMMY):
+                nc.tensor.matmul(scr[:], lhsT=ones_b[:], rhs=mrow[:], start=True, stop=True)
+            dst = hg_w[:, g, 2 * tp * P:2 * (tp + 1) * P, :].rearrange("p (s r) u -> p s r u", s=2)
+            if b in EVAC_V:
+                nc.vector.tensor_copy(out=dst, in_=xt[:].rearrange("p s u r -> p s r u"))
+            else:
+                nc.scalar.copy(out=dst, in_=xt[:].rearrange("p s u r -> p s r u"))
+
+        def quantize_h(g0, g1):
+            nc.vector.quantize_mx(
+                out=hcodes[:, g0:g1, :].rearrange("p g n -> p (g n)").bitcast(FP8X4),
+                scales=hscales[:, g0:g1, :].rearrange("p g n -> p (g n)"),
+                in_=hg[:, g0:g1, :, :].rearrange("p g n t -> p (g n t)"),
+            )
+
+        wf_g = head.tile([P, H, 4], BF16, name="wf_g", align_bytes=64)
+        fcodes = head.tile([P, H], U32, name="fcodes", align_bytes=64)
+        fscales = head.tile([P, H], U8, name="fscales", align_bytes=64)
+        bias_sb = const.tile([P, P], F32, name="bias_sb")
+        mask2 = const.tile([P, NODES], F32, name="mask2")
+        fi2 = head.tile([P, JT, NODES], F32, name="fi2")
+
+        def task_x():
+            turn(NG, 0)
+            turn(NG, 1)
+
+        def task_wf():
+            nc.vector.tensor_copy(
+                out=wf_g[:, 0:V_WF, :].rearrange("p (c i) t -> p c t i", i=4),
+                in_=wf_raw[:, :, 0:V_WF].rearrange("p t (c i) -> p c t i", i=4))
+            nc.scalar.copy(
+                out=wf_g[:, V_WF:H, :].rearrange("p (c i) t -> p c t i", i=4),
+                in_=wf_raw[:, :, V_WF:H].rearrange("p t (c i) -> p c t i", i=4))
+
+        def task_consts():
+            pb = psum.tile([P, P], BF16, name="pb", tag="o0")
+            nc.tensor.transpose(pb[:], brow[:], ident_b[:])
+            nc.vector.tensor_copy(out=bias_sb[:], in_=pb[:])
+            pm = psum.tile([P, NODES], F32, name="pm", tag="o1")
+            nc.tensor.matmul(pm[:], lhsT=ones_b[:], rhs=mrow[:], start=True, stop=True)
+            nc.scalar.activation(out=mask2[:], in_=pm[:], func=ACT.Copy, scale=2.0)
+
+        def task_qxf():
+            quantize_h(NG, NG + 1)
+            nc.vector.quantize_mx(
+                out=fcodes[:].bitcast(FP8X4), scales=fscales[:], in_=wf_g[:].rearrange("p w j -> p (w j)"))
+
+        def task_fi():
+            accfs = {}
+
+            def fi_mx(jt):
+                cols = slice(jt * P, (jt + 1) * P)
+                accf = psum.tile([P, NODES], F32, name="accf", tag="o%d" % (jt % 3))
+                nc.tensor.matmul_mx(
+                    out=accf[:], lhsT=fcodes[:, cols].bitcast(FP8X4), lhsT_scale=fscales[:, cols],
+                    rhs=hcodes[:, NG, :].bitcast(FP8X4), rhs_scale=hscales[:, NG, :], start=True, stop=True,
+                )
+                accfs[jt] = accf
+
+            for jt in range(3):
+                fi_mx(jt)
+            for jt in range(JT):
+                nc.vector.scalar_tensor_tensor(
+                    out=fi2[:, jt, :], in0=accfs[jt][:], scalar=bias_sb[:, TILES + jt:TILES + jt + 1], in1=mask2[:],
+                    op0=ALU.add, op1=ALU.mult,
+                )
+                if jt == 0:
+                    fi_mx(3)
+
+        def task_h0():
+            for g in range(NG):
+                turn(g, 0)
+
+        def task_h1():
+            for g in range(NG):
+                turn(g, 1)
+
+        def task_qh01():
+            quantize_h(0, 2)
+
+        def task_qh23():
+            quantize_h(2, 4)
+
+        def task_qh4():
+            quantize_h(4, 5)
+
+        tasks = {"x": task_x, "wf": task_wf, "consts": task_consts, "qxf": task_qxf, "fi": task_fi, "h0": task_h0,
+                 "h1": task_h1, "qh01": task_qh01, "qh23": task_qh23, "qh4": task_qh4}
+        hooks = {(2, 0): ("x", "wf", "qxf", "consts", "fi", "h0"), (3, 0): ("h1", "qh01", "qh23", "qh4")}
+
+        def spread(eng, out, in_):
+            if eng == "v":
+                nc.vector.tensor_copy(out=out, in_=in_)
+            elif eng == "s":
+                nc.scalar.copy(out=out, in_=in_)
+            else:
+                nc.gpsimd.tensor_scalar(out=out, in0=in_, scalar1=1.0, scalar2=0.0, op0=ALU.mult, op1=ALU.add)
+
+        def interleave_part(u, eng):
+            if u < n_chunk_units:
+                c, g0, ng = units[u]
+                raw = raws[u]
+                a = V_SHARE[c] * ng
+                b = a + G_SHARE[c] * ng
+                if u not in groups:
+                    wg = wg_pool.tile([P, 2 * H, 4], BF16, name="wg", align_bytes=64)
+                    groups[u] = wg
+                wg = groups[u]
+                lo, hi = {"v": (0, a), "g": (a, b), "s": (b, ng * H)}[eng]
+                if hi > lo:
+                    spread(
+                        eng, wg[:, lo:hi, :].rearrange("p (c i) t -> p c t i", i=4),
+                        raw[:, :, lo:hi].rearrange("p t (c i) -> p c t i", i=4))
+            else:
+                base = (u - n_chunk_units) * P
+                raw = raws["last"]
+                a = V_LAST
+                b = a + G_LAST
+                if u not in groups:
+                    wg = wg_pool.tile([P, NG, P, 4], BF16, name="wg", align_bytes=64)
+                    groups[u] = wg
+                wg = groups[u]
+                if eng == "v":
+                    spread(eng, wg[:, 0:4, 0:a, :], raw[:, 0:4, :, base:base + a].rearrange("p g j w -> p g w j"))
+                elif eng == "g":
+                    if b > a:
+                        spread(eng, wg[:, :, a:b, :], raw[:, :, :, base + a:base + b].rearrange("p g j w -> p g w j"))
+                else:
+                    spread(eng, wg[:, :, b:P, :], raw[:, :, :, base + b:base + P].rearrange("p g j w -> p g w j"))
+                    spread(eng, wg[:, 4, 0:a, :], raw[:, 4, :, base:base + a].rearrange("p j w -> p w j"))
+
+        def first_columns(u):
+            if u < n_chunk_units:
+                return groups[u][:, 0:P, :].rearrange("p w j -> p (w j)")
+            return groups[u][:, 0, :, :].rearrange("p w j -> p (w j)")
+
+        def quantize_part(wc, ws, wg, q0, q1):
+            nc.vector.quantize_mx(
+                out=wc[:, q0:q1, :].rearrange("p q w -> p (q w)").bitcast(FP8X4),
+                scales=ws[:, q0:q1, :].rearrange("p q w -> p (q w)"),
+                in_=wg[:, q0:q1, :, :].rearrange("p q w j -> p (q w j)"),
+            )
+
+        def quantize_unit(u):
+            wg = groups[u]
+            if u < n_chunk_units:
+                c, g0, ng = units[u]
+                wc = wc_pool.tile([P, 2 * H], U32, name="wc", align_bytes=64)
+                ws = wc_pool.tile([P, 2 * H], U8, name="ws", align_bytes=64)
+                nc.vector.quantize_mx(
+                    out=wc[:, 0:ng * H].bitcast(FP8X4), scales=ws[:, 0:ng * H],
+                    in_=wg[:, 0:ng * H, :].rearrange("p w j -> p (w j)"))
+            else:
+                wc = wc_pool.tile([P, NG, P], U32, name="wc", align_bytes=64)
+                ws = wc_pool.tile([P, NG, P], U8, name="ws", align_bytes=64)
+                quantize_part(wc, ws, wg, 0, 4)
+                quantize_part(wc, ws, wg, 4, 5)
+            codes[u] = (wc, ws)
+
+        def stationary(s, g):
+            c, jt = divmod(s, JT)
+            if c < NCH - 1:
+                u, i = unit_of[(c, g)]
+                wc, ws = codes[u]
+                cols = slice(i * H + jt * P, i * H + (jt + 1) * P)
+                return wc[:, cols], ws[:, cols]
+            wc, ws = codes[n_chunk_units + jt]
+            return wc[:, g, :], ws[:, g, :]
+
+        accs = {}
+        ncTs = {}
+        fs = {}
+        prods = {}
+        o_acc = []
+
+        def pieces(s):
+            if s >= TILES - N_HALVED:
+                return (slice(0, NODES // 2), slice(NODES // 2, NODES))
+            return (slice(0, NODES),)
+
+        def mx_pass(s, g):
+            lhsT, lhsT_scale = stationary(s, g)
+            nc.tensor.matmul_mx(
+                out=accs[s][:], lhsT=lhsT.bitcast(FP8X4), lhsT_scale=lhsT_scale,
+                rhs=hcodes[:, g, :].bitcast(FP8X4), rhs_scale=hscales[:, g, :],
+                start=(g == 0), stop=(g == NG - 1),
+            )
+
+        def gate(s):
+            jt = s % JT
+            z = z_pool.tile([P, NODES], F32, name="z")
+            f = f_pool.tile([P, NODES], F32, name="f")
+            for cols in pieces(s):
+                nc.vector.tensor_tensor(out=z[:, cols], in0=accs[s][:, cols], in1=fi2[:, jt, cols], op=ALU.add)
+            for cols in pieces(s):
+                nc.scalar.activation(
+                    out=f[:, cols], in_=z[:, cols], func=ACT.Sigmoid, bias=bias_sb[:, s:s + 1], scale=1.0)
+            fs[s] = f
+
+        def turn_nc(s):
+            c, jt = divmod(s, JT)
+            ncT = psum.tile([P, NODES], BF16, name="ncT", tag="t%d" % (s % 2))
+            for t in range(NT):
+                nc.tensor.transpose(ncT[:, t * P:(t + 1) * P], ncs[c][:, t, jt * P:(jt + 1) * P], ident_b[:])
+            ncTs[s] = ncT
+
+        def mult(s):
+            prod = pr_pool.tile([P, NODES], F32, name="prod")
+            for cols in pieces(s):
+                nc.vector.tensor_tensor(out=prod[:, cols], in0=fs[s][:, cols], in1=ncTs[s][:, cols], op=ALU.mult)
+            prods[s] = prod
+
+        def add_up(s):
+            jt = s % JT
+            if s == 0:
+                for t in range(NT):
+                    o_t = psum.tile([P, H], F32, name="o_acc%d" % t, tag="o%d" % t)
+                    o_acc.append(o_t)
+            for t in range(NT):
+                nc.tensor.matmul(
+                    o_acc[t][:, jt * P:(jt + 1) * P], lhsT=prods[s][:, t * P:(t + 1) * P], rhs=ident_f[:],
+                    is_transpose=True, start=(s == 0), stop=(s == TILES - 1),
+                )
+
+        n_mx = 0
+        n_gate = 0
+        n_mult = 0
+        n_nc = 0
+        ready = 0
+        step = 0
+        c0_pass = 0
+        while n_mult < TILES:
+            if 5 <= step + AHEAD < n_units:
+                load_unit(step + AHEAD)
+            old_mx, old_gate = n_mx, n_gate
+            if step in QFIRST:
+                quantize_unit(step - 1)
+            for name in hooks.get((step, 0), ()):
+                tasks[name]()
+            if step < LOOK_FROM:
+                interleave_part(step, "g")
+                interleave_part(step, "s")
+            if step < n_units:
+                interleave_part(step, "v")
+            for name in hooks.get((step, 1), ()):
+                tasks[name]()
+            for r in range(HEAD_DUMMY.get(step, 0)):
+                nc.tensor.matmul(scr[:], lhsT=ones_b[:], rhs=raws[step][:, 0, 0:H], start=True, stop=True)
+            if 1 <= step <= n_units and step not in QFIRST:
+                quantize_unit(step - 1)
+            if LOOK_FROM <= step + 1 < n_units:
+                interleave_part(step + 1, "g")
+                interleave_part(step + 1, "s")
+            if 1 <= step <= n_units:
+                u = step - 1
+                if u < n_chunk_units:
+                    c, g0, ng = units[u]
+                    if g0 == 4:
+                        ready = JT * (c + 1)
+                else:
+                    ready += 1
+            for r in range(2):
+                if n_gate < old_mx:
+                    gate(n_gate)
+                    n_gate += 1
+            first_mult = n_mult
+            for r in range(2):
+                if n_mult < min(old_gate, n_nc):
+                    mult(n_mult)
+                    n_mult += 1
+            for name in hooks.get((step, 2), ()):
+                tasks[name]()
+            if step >= 5 and c0_pass < NG:
+                if c0_pass == 0:
+                    for jt in range(JT):
+                        acc0 = psum.tile([P, NODES], F32, name="acc0", tag="o%d" % jt)
+                        accs[jt] = acc0
+                while c0_pass < min(NG, step):
+                    for jt in range(JT):
+                        mx_pass(jt, c0_pass)
+                    c0_pass += 1
+                if c0_pass == NG:
+                    n_mx = JT
+            for r in range(2):
+                if JT <= n_mx < ready and n_gate >= n_mx - 1 and n_gate >= JT:
+                    acc = psum.tile([P, NODES], F32, name="acc", tag="a%d" % (n_mx % 2))
+                    accs[n_mx] = acc
+                    for g in range(NG):
+                        mx_pass(n_mx, g)
+                    n_mx += 1
+            if BOUND_DUMMY and n_mx == old_mx and (n_gate == n_mx or n_mx == JT) and JT <= n_mx < TILES and step < n_units:
+                scr2 = psum.tile([P, NODES], F32, name="scr2", tag="a%d" % (n_mx % 2))
+                for r in range(BOUND_DUMMY):
+                    nc.tensor.matmul(scr2[:], lhsT=ones_b[:], rhs=first_columns(step), start=True, stop=True)
+            for r in range(2):
+                if n_nc < n_mx and n_mult >= n_nc - 1:
+                    turn_nc(n_nc)
+                    n_nc += 1
+            for s in range(first_mult, n_mult):
+                add_up(s)
+            step += 1
+
+        o32s = []
+        o8s = []
+        for t in range(NT):
+            o32 = out_pool.tile([P, H], F32, name="o32")
+            o32s.append(o32)
+            o8 = out_pool.tile([P, H], FP8, name="o8")
+            o8s.append(o8)
+        def put(eng, kind, t):
+            rows = slice(t * P, (t + 1) * P)
+            if kind == "f":
+                if eng == "v":
+                    nc.vector.tensor_copy(out=o32s[t][:], in_=o_acc[t][:])
+                else:
+                    nc.scalar.copy(out=o32s[t][:], in_=o_acc[t][:])
+                nc.sync.dma_start(out=out_0[rows, :], in_=o32s[t][:])
+            else:
+                if eng == "v":
+                    nc.vector.tensor_scalar(
+                        out=o8s[t][:], in0=o_acc[t][:], scalar1=Y_SCALE, scalar2=None, op0=ALU.mult, saturate=False)
+                else:
+                    nc.scalar.activation(out=o8s[t][:], in_=o_acc[t][:], func=ACT.Copy, scale=Y_SCALE, saturate=False)
+                nc.sync.dma_start(out=out_1[rows, :], in_=o8s[t][:].bitcast(U8))
+
+        for i in range(max(len(OUT_V), len(OUT_S))):
+            if i < len(OUT_S):
+                put("s", OUT_S[i][0], OUT_S[i][1])
+            if i < len(OUT_V):
+                put("v", OUT_V[i][0], OUT_V[i][1])

@@ -24,10 +24,10 @@ NG = 5
 TILES = NCH * JT
 Y_SCALE = 160.0
 V_WF = 256
-V_SHARE = (256, 160, 160, 160)
-G_SHARE = (0, 0, 0, 0)
-G_LAST = 0
-V_LAST = 48
+V_SHARE = (192, 64, 64, 64)
+G_SHARE = (128, 128, 128, 128)
+G_LAST = 32
+V_LAST = 16
 AHEAD = 4
 EVAC_V = (0, 2, 4, 6, 8, 10)
 MANUAL = False
@@ -262,7 +262,9 @@ def tile_treelstmcell_pa_kernel(
                     groups[u] = wg
                 wg = groups[u]
                 lo, hi = {"v": (0, a), "g": (a, b), "s": (b, ng * H)}[eng]
-                if hi > lo:
+                if hi > lo and eng == "g":
+                    spread(eng, wg[:, lo:hi, :], raw[:, :, lo:hi].rearrange("p t c -> p c t"))
+                elif hi > lo:
                     spread(
                         eng, wg[:, lo:hi, :].rearrange("p (c i) t -> p c t i", i=4),
                         raw[:, :, lo:hi].rearrange("p t (c i) -> p c t i", i=4))

@@ -39,6 +39,7 @@ OUT_S = (("f", 0), ("f", 1), ("f", 2), ("f", 3))
 TURN_DUMMY = 0
 HEAD_DUMMY = {0: 2, 1: 2, 2: 2, 3: 2, 4: 2}
 BOUND_DUMMY = 4
+RUN = 8
 
 
 def tile_treelstmcell_pa_kernel(
@@ -181,11 +182,11 @@ def tile_treelstmcell_pa_kernel(
 
         def task_wf():
             nc.vector.tensor_copy(
-                out=wf_g[:, 0:V_WF, :].rearrange("p (c i) t -> p c t i", i=4),
-                in_=wf_raw[:, :, 0:V_WF].rearrange("p t (c i) -> p c t i", i=4))
+                out=wf_g[:, 0:V_WF, :].rearrange("p (c i) t -> p c t i", i=RUN),
+                in_=wf_raw[:, :, 0:V_WF].rearrange("p t (c i) -> p c t i", i=RUN))
             nc.scalar.copy(
-                out=wf_g[:, V_WF:H, :].rearrange("p (c i) t -> p c t i", i=4),
-                in_=wf_raw[:, :, V_WF:H].rearrange("p t (c i) -> p c t i", i=4))
+                out=wf_g[:, V_WF:H, :].rearrange("p (c i) t -> p c t i", i=RUN),
+                in_=wf_raw[:, :, V_WF:H].rearrange("p t (c i) -> p c t i", i=RUN))
 
         def task_consts():
             pb = psum.tile([P, P], BF16, name="pb", tag="o0")
@@ -266,8 +267,8 @@ def tile_treelstmcell_pa_kernel(
                     spread(eng, wg[:, lo:hi, :], raw[:, :, lo:hi].rearrange("p t c -> p c t"))
                 elif hi > lo:
                     spread(
-                        eng, wg[:, lo:hi, :].rearrange("p (c i) t -> p c t i", i=4),
-                        raw[:, :, lo:hi].rearrange("p t (c i) -> p c t i", i=4))
+                        eng, wg[:, lo:hi, :].rearrange("p (c i) t -> p c t i", i=RUN),
+                        raw[:, :, lo:hi].rearrange("p t (c i) -> p c t i", i=RUN))
             else:
                 base = (u - n_chunk_units) * P
                 raw = raws["last"]

@@ -24,10 +24,11 @@ NG = 5
 TILES = NCH * JT
 Y_SCALE = 160.0
 V_WF = 256
-V_SHARE = (192, 64, 64, 64)
+V_HEAD = 192
+V_FIRST = 320
 G_SHARE = (128, 128, 128, 128)
-G_LAST = 32
-V_LAST = 16
+G_LAST = 40
+V_LAST = 0
 AHEAD = 4
 EVAC_V = (0, 2, 4, 6, 8, 10)
 MANUAL = False
@@ -37,8 +38,8 @@ N_HALVED = 1
 OUT_V = (("b", 2), ("b", 3), ("b", 0), ("b", 1))
 OUT_S = (("f", 0), ("f", 1), ("f", 2), ("f", 3))
 TURN_DUMMY = 0
-HEAD_DUMMY = {0: 2, 1: 2, 2: 2, 3: 2, 4: 2}
-BOUND_DUMMY = 4
+HEAD_DUMMY = {}
+BOUND_DUMMY = 0
 RUN = 8
 
 
@@ -53,9 +54,9 @@ def tile_treelstmcell_pa_kernel(
         wg_pool = ctx.enter_context(tc.tile_pool(name="wg", bufs=3))
         wc_pool = ctx.enter_context(tc.tile_pool(name="wc", bufs=7))
         nc_pool = ctx.enter_context(tc.tile_pool(name="ncp", bufs=4))
-        z_pool = ctx.enter_context(tc.tile_pool(name="zp", bufs=3))
-        f_pool = ctx.enter_context(tc.tile_pool(name="fp", bufs=4))
-        pr_pool = ctx.enter_context(tc.tile_pool(name="prp", bufs=3))
+        z_pool = ctx.enter_context(tc.tile_pool(name="zp", bufs=2))
+        f_pool = ctx.enter_context(tc.tile_pool(name="fp", bufs=2))
+        pr_pool = ctx.enter_context(tc.tile_pool(name="prp", bufs=2))
         out_pool = ctx.enter_context(tc.tile_pool(name="outp", bufs=4))
         psum = ctx.enter_context(tc.psum_pool(name="psum", bufs=1))
         if MANUAL:
@@ -256,7 +257,7 @@ def tile_treelstmcell_pa_kernel(
             if u < n_chunk_units:
                 c, g0, ng = units[u]
                 raw = raws[u]
-                a = V_SHARE[c] * ng
+                a = V_HEAD * ng if c == 0 else (V_FIRST if g0 == 0 else 0)
                 b = a + G_SHARE[c] * ng
                 if u not in groups:
                     wg = wg_pool.tile([P, 2 * H, 4], BF16, name="wg", align_bytes=64)
@@ -279,13 +280,15 @@ def tile_treelstmcell_pa_kernel(
                     groups[u] = wg
                 wg = groups[u]
                 if eng == "v":
-                    spread(eng, wg[:, 0:4, 0:a, :], raw[:, 0:4, :, base:base + a].rearrange("p g j w -> p g w j"))
+                    if a > 0:
+                        spread(eng, wg[:, 0:4, 0:a, :], raw[:, 0:4, :, base:base + a].rearrange("p g j w -> p g w j"))
                 elif eng == "g":
                     if b > a:
                         spread(eng, wg[:, :, a:b, :], raw[:, :, :, base + a:base + b].rearrange("p g j w -> p g w j"))
                 else:
                     spread(eng, wg[:, :, b:P, :], raw[:, :, :, base + b:base + P].rearrange("p g j w -> p g w j"))
-                    spread(eng, wg[:, 4, 0:a, :], raw[:, 4, :, base:base + a].rearrange("p j w -> p w j"))
+                    if a > 0:
+                        spread(eng, wg[:, 4, 0:a, :], raw[:, 4, :, base:base + a].rearrange("p j w -> p w j"))
 
         def first_columns(u):
             if u < n_chunk_units:
@@ -330,6 +333,7 @@ def tile_treelstmcell_pa_kernel(
         fs = {}
         prods = {}
         o_acc = []
+        nc_calls = []
 
         def pieces(s):
             if s >= TILES - N_HALVED:
@@ -344,29 +348,48 @@ def tile_treelstmcell_pa_kernel(
                 start=(g == 0), stop=(g == NG - 1),
             )
 
-        def gate(s):
-            jt = s % JT
-            z = z_pool.tile([P, NODES], F32, name="z")
-            f = f_pool.tile([P, NODES], F32, name="f")
-            for cols in pieces(s):
-                nc.vector.tensor_tensor(out=z[:, cols], in0=accs[s][:, cols], in1=fi2[:, jt, cols], op=ALU.add)
-            for cols in pieces(s):
+        def gate(tiles):
+            z = z_pool.tile([P, 2, NODES], F32, name="z")
+            f = f_pool.tile([P, 2, NODES], F32, name="f")
+            for i in range(len(tiles)):
+                s = tiles[i]
+                for cols in pieces(s):
+                    nc.vector.scalar_tensor_tensor(
+                        out=z[:, i, cols], in0=accs[s][:, cols], scalar=bias_sb[:, s:s + 1], in1=fi2[:, s % JT, cols],
+                        op0=ALU.add, op1=ALU.add)
+                fs[s] = (f, i, tiles[0])
+            if len(tiles) == 2:
                 nc.scalar.activation(
-                    out=f[:, cols], in_=z[:, cols], func=ACT.Sigmoid, bias=bias_sb[:, s:s + 1], scale=1.0)
-            fs[s] = f
+                    out=f[:].rearrange("p a n -> p (a n)"), in_=z[:].rearrange("p a n -> p (a n)"), func=ACT.Sigmoid)
+            else:
+                for cols in pieces(tiles[0]):
+                    nc.scalar.activation(out=f[:, 0, cols], in_=z[:, 0, cols], func=ACT.Sigmoid)
 
-        def turn_nc(s):
-            c, jt = divmod(s, JT)
-            ncT = psum.tile([P, NODES], BF16, name="ncT", tag="t%d" % (s % 2))
-            for t in range(NT):
-                nc.tensor.transpose(ncT[:, t * P:(t + 1) * P], ncs[c][:, t, jt * P:(jt + 1) * P], ident_b[:])
-            ncTs[s] = ncT
+        def turn_nc(tiles):
+            ncT = psum.tile([P, 2, NODES], BF16, name="ncT", tag="t0")
+            for i in range(len(tiles)):
+                c, jt = divmod(tiles[i], JT)
+                for t in range(NT):
+                    nc.tensor.transpose(ncT[:, i, t * P:(t + 1) * P], ncs[c][:, t, jt * P:(jt + 1) * P], ident_b[:])
+                ncTs[tiles[i]] = (ncT, i, tiles[0])
+            nc_calls.append(tiles[-1])
 
-        def mult(s):
-            prod = pr_pool.tile([P, NODES], F32, name="prod")
-            for cols in pieces(s):
-                nc.vector.tensor_tensor(out=prod[:, cols], in0=fs[s][:, cols], in1=ncTs[s][:, cols], op=ALU.mult)
-            prods[s] = prod
+        def mult(tiles):
+            prod = pr_pool.tile([P, 2, NODES], F32, name="prod")
+            for i in range(len(tiles)):
+                prods[tiles[i]] = (prod, i)
+            s = tiles[0]
+            if len(tiles) == 2 and fs[s][2] == s and fs[s + 1][2] == s and ncTs[s][2] == s and ncTs[s + 1][2] == s:
+                nc.vector.tensor_tensor(
+                    out=prod[:].rearrange("p a n -> p (a n)"), in0=fs[s][0][:].rearrange("p a n -> p (a n)"),
+                    in1=ncTs[s][0][:].rearrange("p a n -> p (a n)"), op=ALU.mult)
+            else:
+                for i in range(len(tiles)):
+                    s = tiles[i]
+                    for cols in pieces(s):
+                        nc.vector.tensor_tensor(
+                            out=prod[:, i, cols], in0=fs[s][0][:, fs[s][1], cols], in1=ncTs[s][0][:, ncTs[s][1], cols],
+                            op=ALU.mult)
 
         def add_up(s):
             jt = s % JT
@@ -376,7 +399,7 @@ def tile_treelstmcell_pa_kernel(
                     o_acc.append(o_t)
             for t in range(NT):
                 nc.tensor.matmul(
-                    o_acc[t][:, jt * P:(jt + 1) * P], lhsT=prods[s][:, t * P:(t + 1) * P], rhs=ident_f[:],
+                    o_acc[t][:, jt * P:(jt + 1) * P], lhsT=prods[s][0][:, prods[s][1], t * P:(t + 1) * P], rhs=ident_f[:],
                     is_transpose=True, start=(s == 0), stop=(s == TILES - 1),
                 )
 
@@ -417,15 +440,15 @@ def tile_treelstmcell_pa_kernel(
                         ready = JT * (c + 1)
                 else:
                     ready += 1
-            for r in range(2):
-                if n_gate < old_mx:
-                    gate(n_gate)
-                    n_gate += 1
+            todo = list(range(n_gate, min(n_gate + 2, old_mx)))
+            if todo:
+                gate(todo)
+                n_gate += len(todo)
             first_mult = n_mult
-            for r in range(2):
-                if n_mult < min(old_gate, n_nc):
-                    mult(n_mult)
-                    n_mult += 1
+            todo = list(range(n_mult, min(n_mult + 2, old_gate, n_nc)))
+            if todo:
+                mult(todo)
+                n_mult += len(todo)
             for name in hooks.get((step, 2), ()):
                 tasks[name]()
             if step >= 5 and c0_pass < NG:
@@ -440,8 +463,8 @@ def tile_treelstmcell_pa_kernel(
                 if c0_pass == NG:
                     n_mx = JT
             for r in range(2):
-                if JT <= n_mx < ready and n_gate >= n_mx - 1 and n_gate >= JT:
-                    acc = psum.tile([P, NODES], F32, name="acc", tag="a%d" % (n_mx % 2))
+                if JT <= n_mx < ready and n_gate >= n_mx - 2 and n_gate >= JT:
+                    acc = psum.tile([P, NODES], F32, name="acc", tag=("a0", "a1", "t1")[n_mx % 3])
                     accs[n_mx] = acc
                     for g in range(NG):
                         mx_pass(n_mx, g)
@@ -450,10 +473,10 @@ def tile_treelstmcell_pa_kernel(
                 scr2 = psum.tile([P, NODES], F32, name="scr2", tag="a%d" % (n_mx % 2))
                 for r in range(BOUND_DUMMY):
                     nc.tensor.matmul(scr2[:], lhsT=ones_b[:], rhs=first_columns(step), start=True, stop=True)
-            for r in range(2):
-                if n_nc < n_mx and n_mult >= n_nc - 1:
-                    turn_nc(n_nc)
-                    n_nc += 1
+            todo = list(range(n_nc, min(n_nc + 2, n_mx)))
+            if todo and (len(nc_calls) < 1 or n_mult > nc_calls[-1]):
+                turn_nc(todo)
+                n_nc += len(todo)
             for s in range(first_mult, n_mult):
                 add_up(s)
             step += 1

@@ -30,7 +30,7 @@ G_SHARE = (128, 128, 128, 128)
 G_LAST = 40
 V_LAST = 0
 AHEAD = 4
-EVAC_V = (0, 2, 4, 6, 8, 10)
+EVAC_V = (0, 4, 8)
 MANUAL = False
 QFIRST = (2, 3, 4)
 LOOK_FROM = 5

@@ -370,7 +370,9 @@ def tile_treelstmcell_pa_kernel(
             for i in range(len(tiles)):
                 c, jt = divmod(tiles[i], JT)
                 for t in range(NT):
-                    nc.tensor.transpose(ncT[:, i, t * P:(t + 1) * P], ncs[c][:, t, jt * P:(jt + 1) * P], ident_b[:])
+                    nc.tensor.matmul(
+                        ncT[:, i, t * P:(t + 1) * P], lhsT=ncs[c][:, t, jt * P:(jt + 1) * P], rhs=ident_b[:],
+                        start=True, stop=True)
                 ncTs[tiles[i]] = (ncT, i, tiles[0])
             nc_calls.append(tiles[-1])
 

from contextlib import ExitStack

import concourse.mybir as mybir
from concourse.masks import make_identity

FLOPS = 2 * 512 * 2560 * 2560 + 2 * 512 * 512 * 512

F32 = mybir.dt.float32
BF16 = mybir.dt.bfloat16
U32 = mybir.dt.uint32
U8 = mybir.dt.uint8
FP8X4 = mybir.dt.float8_e4m3fn_x4
FP8 = mybir.dt.float8_e4m3fn
ACT = mybir.ActivationFunctionType
ALU = mybir.AluOpType

P = 128
NODES = 512
NT = 4
NCH = 5
H = 512
JT = 4
NG = 5
TILES = NCH * JT
Y_SCALE = 160.0
V_WF = 256
V_HEAD = 192
V_FIRST = 320
G_SHARE = (128, 128, 128, 128)
G_LAST = 40
V_LAST = 0
AHEAD = 4
EVAC_V = (0, 4, 8)
MANUAL = False
QFIRST = (2, 3, 4)
LOOK_FROM = 5
N_HALVED = 1
OUT_V = (("b", 2), ("b", 3), ("b", 0), ("b", 1))
OUT_S = (("f", 0), ("f", 1), ("f", 2), ("f", 3))
TURN_DUMMY = 0
HEAD_DUMMY = {}
BOUND_DUMMY = 0
RUN = 8


def tile_treelstmcell_pa_kernel(
    tc, x, x_mask, neighbour_h, neighbour_c, W_f_in, b_f_in, W_aggr_f, b_aggr_f, out_0, out_1
):
    nc = tc.nc
    with ExitStack() as ctx:
        const = ctx.enter_context(tc.tile_pool(name="const", bufs=1))
        head = ctx.enter_context(tc.tile_pool(name="head", bufs=1))
        wraw_pool = ctx.enter_context(tc.tile_pool(name="wraw", bufs=AHEAD + 1))
        wg_pool = ctx.enter_context(tc.tile_pool(name="wg", bufs=3))
        wc_pool = ctx.enter_context(tc.tile_pool(name="wc", bufs=7))
        nc_pool = ctx.enter_context(tc.tile_pool(name="ncp", bufs=4))
        z_pool = ctx.enter_context(tc.tile_pool(name="zp", bufs=2))
        f_pool = ctx.enter_context(tc.tile_pool(name="fp", bufs=2))
        pr_pool = ctx.enter_context(tc.tile_pool(name="prp", bufs=2))
        out_pool = ctx.enter_context(tc.tile_pool(name="outp", bufs=4))
        psum = ctx.enter_context(tc.psum_pool(name="psum", bufs=1))
        if MANUAL:
            ctx.enter_context(tc.manual_schedule())

        warm = const.tile([P, 2], F32, name="warm")
        nc.vector.memset(warm[:], 0.0)
        nc.scalar.activation(out=warm[:, 1:2], in_=warm[:, 0:1], func=ACT.Sigmoid)

        ident_f = const.tile([P, P], F32, name="ident_f")
        make_identity(nc, ident_f[:])
        brow = const.tile([P, P], BF16, name="brow")
        nc.vector.memset(brow[:], 0.0)
        mrow = const.tile([P, NODES], BF16, name="mrow")
        nc.vector.memset(mrow[:], 0.0)
        ident_b = const.tile([P, P], BF16, name="ident_b")
        make_identity(nc, ident_b[:])
        ones_b = const.tile([P, P], BF16, name="ones_b")
        nc.vector.memset(ones_b[:], 1.0)

        units = [(0, g, 1) for g in range(NG)]
        units += [(c, g0, ng) for c in range(1, NCH - 1) for (g0, ng) in ((0, 2), (2, 2), (4, 1))]
        n_chunk_units = len(units)
        n_units = n_chunk_units + JT
        unit_of = {}
        for u in range(n_chunk_units):
            for i in range(units[u][2]):
                unit_of[(units[u][0], units[u][1] + i)] = (u, i)
        raws = {}
        groups = {}
        codes = {}
        ncs = {}

        def w_chunk(c, g):
            return W_aggr_f[512 * g:512 * (g + 1), H * c:H * (c + 1)].rearrange("(p j) w -> p j w", j=4)

        def load_nc(c):
            nct = nc_pool.tile([P, NT, H], BF16, name="nct")
            nc.sync.dma_start(out=nct[:], in_=neighbour_c[:, c, :].rearrange("(t p) h -> p t h", p=P))
            ncs[c] = nct

        def load_unit(u):
            if u < n_chunk_units:
                c, g0, ng = units[u]
                raw = wraw_pool.tile([P, 4, 2 * H], BF16, name="wraw")
                for i in range(ng):
                    nc.sync.dma_start(out=raw[:, :, i * H:(i + 1) * H], in_=w_chunk(c, g0 + i))
                raws[u] = raw
                if g0 == 4:
                    load_nc(c)
            elif u == n_chunk_units:
                raw = head.tile([P, NG, 4, H], BF16, name="w4raw", tag="big", align_bytes=64)
                for g in range(NG):
                    nc.sync.dma_start(out=raw[:, g, :, :], in_=w_chunk(NCH - 1, g))
                raws["last"] = raw
                load_nc(NCH - 1)

        x_sb = head.tile([P, NT, 512], BF16, name="x_sb")
        wf_raw = head.tile([P, 4, H], BF16, name="wf_raw")
        hf = neighbour_h.rearrange("n c h -> n (c h)")
        nh_sb = []
        for t in range(NT):
            nh_t = head.tile([P, NCH * H], BF16, name="nh%d" % t)
            nh_sb.append(nh_t)
        for item in (0, 1, "small", "x", "wf", -1, -2, 2, -3, -4, 3, 4):
            if item == "small":
                nc.sync.dma_start(out=brow[0:20, :], in_=b_aggr_f.rearrange("(r p) -> r p", p=P))
                nc.sync.dma_start(out=brow[20:24, :], in_=b_f_in.rearrange("(r p) -> r p", p=P))
                nc.sync.dma_start(out=mrow[0:1, :], in_=x_mask.rearrange("(o n) -> o n", o=1))
            elif item == "x":
                nc.sync.dma_start(out=x_sb[:], in_=x.rearrange("(t p) k -> p t k", p=P))
            elif item == "wf":
                nc.sync.dma_start(out=wf_raw[:], in_=W_f_in.rearrange("(p j) w -> p j w", j=4))
            elif item < 0:
                t = -item - 1
                nc.sync.dma_start(out=nh_sb[t][:], in_=hf[t * P:(t + 1) * P, :])
            else:
                load_unit(item)

        hg = head.tile([P, NG + 1, NODES, 4], BF16, name="hg", tag="big", align_bytes=64)
        hg_w = hg[:].bitcast(F32)
        hcodes = head.tile([P, NG + 1, NODES], U32, name="hcodes", align_bytes=64)
        hscales = head.tile([P, NG + 1, NODES], U8, name="hscales", align_bytes=64)
        scr = psum.tile([P, NODES], F32, name="scr", tag="o3")
        banks = [0]

        def turn(g, tp):
            b = banks[0]
            banks[0] += 1
            xt = psum.tile([P, 2, 2, P], F32, name="xt", tag=("t0", "t1", "a0", "a1")[b % 4])
            for s in range(2):
                t = 2 * tp + s
                for u in range(2):
                    if g < NG:
                        src = nh_sb[t][:].bitcast(F32)[:, 256 * g + u:256 * (g + 1):2]
                    else:
                        src = x_sb[:, t, :].bitcast(F32)[:, u:256:2]
                    nc.tensor.transpose(xt[:, s, u, :], src, ident_f[:])
            for r in range(TURN_DUMMY):
                nc.tensor.matmul(scr[:], lhsT=ones_b[:], rhs=mrow[:], start=True, stop=True)
            dst = hg_w[:, g, 2 * tp * P:2 * (tp + 1) * P, :].rearrange("p (s r) u -> p s r u", s=2)
            if b in EVAC_V:
                nc.vector.tensor_copy(out=dst, in_=xt[:].rearrange("p s u r -> p s r u"))
            else:
                nc.scalar.copy(out=dst, in_=xt[:].rearrange("p s u r -> p s r u"))

        def quantize_h(g0, g1):
            nc.vector.quantize_mx(
                out=hcodes[:, g0:g1, :].rearrange("p g n -> p (g n)").bitcast(FP8X4),
                scales=hscales[:, g0:g1, :].rearrange("p g n -> p (g n)"),
                in_=hg[:, g0:g1, :, :].rearrange("p g n t -> p (g n t)"),
            )

        wf_g = head.tile([P, H, 4], BF16, name="wf_g", align_bytes=64)
        fcodes = head.tile([P, H], U32, name="fcodes", align_bytes=64)
        fscales = head.tile([P, H], U8, name="fscales", align_bytes=64)
        bias_sb = const.tile([P, P], F32, name="bias_sb")
        mask2 = const.tile([P, NODES], F32, name="mask2")
        fi2 = head.tile([P, JT, NODES], F32, name="fi2")

        def task_x():
            turn(NG, 0)
            turn(NG, 1)

        def task_wf():
            nc.vector.tensor_copy(
                out=wf_g[:, 0:V_WF, :].rearrange("p (c i) t -> p c t i", i=RUN),
                in_=wf_raw[:, :, 0:V_WF].rearrange("p t (c i) -> p c t i", i=RUN))
            nc.scalar.copy(
                out=wf_g[:, V_WF:H, :].rearrange("p (c i) t -> p c t i", i=RUN),
                in_=wf_raw[:, :, V_WF:H].rearrange("p t (c i) -> p c t i", i=RUN))

        def task_consts():
            pb = psum.tile([P, P], BF16, name="pb", tag="o0")
            nc.tensor.transpose(pb[:], brow[:], ident_b[:])
            nc.vector.tensor_copy(out=bias_sb[:], in_=pb[:])
            pm = psum.tile([P, NODES], F32, name="pm", tag="o1")
            nc.tensor.matmul(pm[:], lhsT=ones_b[:], rhs=mrow[:], start=True, stop=True)
            nc.scalar.activation(out=mask2[:], in_=pm[:], func=ACT.Copy, scale=2.0)

        def task_qxf():
            quantize_h(NG, NG + 1)
            nc.vector.quantize_mx(
                out=fcodes[:].bitcast(FP8X4), scales=fscales[:], in_=wf_g[:].rearrange("p w j -> p (w j)"))

        def task_fi():
            accfs = {}

            def fi_mx(jt):
                cols = slice(jt * P, (jt + 1) * P)
                accf = psum.tile([P, NODES], F32, name="accf", tag="o%d" % (jt % 3))
                nc.tensor.matmul_mx(
                    out=accf[:], lhsT=fcodes[:, cols].bitcast(FP8X4), lhsT_scale=fscales[:, cols],
                    rhs=hcodes[:, NG, :].bitcast(FP8X4), rhs_scale=hscales[:, NG, :], start=True, stop=True,
                )
                accfs[jt] = accf

            for jt in range(3):
                fi_mx(jt)
            for jt in range(JT):
                nc.vector.scalar_tensor_tensor(
                    out=fi2[:, jt, :], in0=accfs[jt][:], scalar=bias_sb[:, TILES + jt:TILES + jt + 1], in1=mask2[:],
                    op0=ALU.add, op1=ALU.mult,
                )
                if jt == 0:
                    fi_mx(3)

        def task_h0():
            for g in range(NG):
                turn(g, 0)

        def task_h1():
            for g in range(NG):
                turn(g, 1)

        def task_qh01():
            quantize_h(0, 2)

        def task_qh23():
            quantize_h(2, 4)

        def task_qh4():
            quantize_h(4, 5)

        tasks = {"x": task_x, "wf": task_wf, "consts": task_consts, "qxf": task_qxf, "fi": task_fi, "h0": task_h0,
                 "h1": task_h1, "qh01": task_qh01, "qh23": task_qh23, "qh4": task_qh4}
        hooks = {(2, 0): ("x", "wf", "qxf", "consts", "fi", "h0"), (3, 0): ("h1", "qh01", "qh23", "qh4")}

        def spread(eng, out, in_):
            if eng == "v":
                nc.vector.tensor_copy(out=out, in_=in_)
            elif eng == "s":
                nc.scalar.copy(out=out, in_=in_)
            else:
                nc.gpsimd.tensor_scalar(out=out, in0=in_, scalar1=1.0, scalar2=0.0, op0=ALU.mult, op1=ALU.add)

        def interleave_part(u, eng):
            if u < n_chunk_units:
                c, g0, ng = units[u]
                raw = raws[u]
                a = V_HEAD * ng if c == 0 else (V_FIRST if g0 == 0 else 0)
                b = a + G_SHARE[c] * ng
                if u not in groups:
                    wg = wg_pool.tile([P, 2 * H, 4], BF16, name="wg", align_bytes=64)
                    groups[u] = wg
                wg = groups[u]
                lo, hi = {"v": (0, a), "g": (a, b), "s": (b, ng * H)}[eng]
                if hi > lo and eng == "g":
                    spread(eng, wg[:, lo:hi, :], raw[:, :, lo:hi].rearrange("p t c -> p c t"))
                elif hi > lo:
                    spread(
                        eng, wg[:, lo:hi, :].rearrange("p (c i) t -> p c t i", i=RUN),
                        raw[:, :, lo:hi].rearrange("p t (c i) -> p c t i", i=RUN))
            else:
                base = (u - n_chunk_units) * P
                raw = raws["last"]
                a = V_LAST
                b = a + G_LAST
                if u not in groups:
                    wg = wg_pool.tile([P, NG, P, 4], BF16, name="wg", align_bytes=64)
                    groups[u] = wg
                wg = groups[u]
                if eng == "v":
                    if a > 0:
                        spread(eng, wg[:, 0:4, 0:a, :], raw[:, 0:4, :, base:base + a].rearrange("p g j w -> p g w j"))
                elif eng == "g":
                    if b > a:
                        spread(eng, wg[:, :, a:b, :], raw[:, :, :, base + a:base + b].rearrange("p g j w -> p g w j"))
                else:
                    spread(eng, wg[:, :, b:P, :], raw[:, :, :, base + b:base + P].rearrange("p g j w -> p g w j"))
                    if a > 0:
                        spread(eng, wg[:, 4, 0:a, :], raw[:, 4, :, base:base + a].rearrange("p j w -> p w j"))

        def first_columns(u):
            if u < n_chunk_units:
                return groups[u][:, 0:P, :].rearrange("p w j -> p (w j)")
            return groups[u][:, 0, :, :].rearrange("p w j -> p (w j)")

        def quantize_part(wc, ws, wg, q0, q1):
            nc.vector.quantize_mx(
                out=wc[:, q0:q1, :].rearrange("p q w -> p (q w)").bitcast(FP8X4),
                scales=ws[:, q0:q1, :].rearrange("p q w -> p (q w)"),
                in_=wg[:, q0:q1, :, :].rearrange("p q w j -> p (q w j)"),
            )

        def quantize_unit(u):
            wg = groups[u]
            if u < n_chunk_units:
                c, g0, ng = units[u]
                wc = wc_pool.tile([P, 2 * H], U32, name="wc", align_bytes=64)
                ws = wc_pool.tile([P, 2 * H], U8, name="ws", align_bytes=64)
                nc.vector.quantize_mx(
                    out=wc[:, 0:ng * H].bitcast(FP8X4), scales=ws[:, 0:ng * H],
                    in_=wg[:, 0:ng * H, :].rearrange("p w j -> p (w j)"))
            else:
                wc = wc_pool.tile([P, NG, P], U32, name="wc", align_bytes=64)
                ws = wc_pool.tile([P, NG, P], U8, name="ws", align_bytes=64)
                quantize_part(wc, ws, wg, 0, 4)
                quantize_part(wc, ws, wg, 4, 5)
            codes[u] = (wc, ws)

        def stationary(s, g):
            c, jt = divmod(s, JT)
            if c < NCH - 1:
                u, i = unit_of[(c, g)]
                wc, ws = codes[u]
                cols = slice(i * H + jt * P, i * H + (jt + 1) * P)
                return wc[:, cols], ws[:, cols]
            wc, ws = codes[n_chunk_units + jt]
            return wc[:, g, :], ws[:, g, :]

        accs = {}
        ncTs = {}
        fs = {}
        prods = {}
        o_acc = []
        nc_calls = []

        def pieces(s):
            if s >= TILES - N_HALVED:
                return (slice(0, NODES // 2), slice(NODES // 2, NODES))
            return (slice(0, NODES),)

        def mx_pass(s, g):
            lhsT, lhsT_scale = stationary(s, g)
            nc.tensor.matmul_mx(
                out=accs[s][:], lhsT=lhsT.bitcast(FP8X4), lhsT_scale=lhsT_scale,
                rhs=hcodes[:, g, :].bitcast(FP8X4), rhs_scale=hscales[:, g, :],
                start=(g == 0), stop=(g == NG - 1),
            )

        def gate(tiles):
            z = z_pool.tile([P, 2, NODES], F32, name="z")
            f = f_pool.tile([P, 2, NODES], F32, name="f")
            for i in range(len(tiles)):
                s = tiles[i]
                for cols in pieces(s):
                    nc.vector.scalar_tensor_tensor(
                        out=z[:, i, cols], in0=accs[s][:, cols], scalar=bias_sb[:, s:s + 1], in1=fi2[:, s % JT, cols],
                        op0=ALU.add, op1=ALU.add)
                fs[s] = (f, i, tiles[0])
            if len(tiles) == 2:
                nc.scalar.activation(
                    out=f[:].rearrange("p a n -> p (a n)"), in_=z[:].rearrange("p a n -> p (a n)"), func=ACT.Sigmoid)
            else:
                for cols in pieces(tiles[0]):
                    nc.scalar.activation(out=f[:, 0, cols], in_=z[:, 0, cols], func=ACT.Sigmoid)

        def turn_nc(tiles):
            ncT = psum.tile([P, 2, NODES], BF16, name="ncT", tag="t0")
            for i in range(len(tiles)):
                c, jt = divmod(tiles[i], JT)
                for t in range(NT):
                    nc.tensor.matmul(
                        ncT[:, i, t * P:(t + 1) * P], lhsT=ncs[c][:, t, jt * P:(jt + 1) * P], rhs=ident_b[:],
                        start=True, stop=True)
                ncTs[tiles[i]] = (ncT, i, tiles[0])
            nc_calls.append(tiles[-1])

        def mult(tiles):
            prod = pr_pool.tile([P, 2, NODES], F32, name="prod")
            for i in range(len(tiles)):
                prods[tiles[i]] = (prod, i)
            s = tiles[0]
            if len(tiles) == 2 and fs[s][2] == s and fs[s + 1][2] == s and ncTs[s][2] == s and ncTs[s + 1][2] == s:
                nc.vector.tensor_tensor(
                    out=prod[:].rearrange("p a n -> p (a n)"), in0=fs[s][0][:].rearrange("p a n -> p (a n)"),
                    in1=ncTs[s][0][:].rearrange("p a n -> p (a n)"), op=ALU.mult)
            else:
                for i in range(len(tiles)):
                    s = tiles[i]
                    for cols in pieces(s):
                        nc.vector.tensor_tensor(
                            out=prod[:, i, cols], in0=fs[s][0][:, fs[s][1], cols], in1=ncTs[s][0][:, ncTs[s][1], cols],
                            op=ALU.mult)

        def add_up(s):
            jt = s % JT
            if s == 0:
                for t in range(NT):
                    o_t = psum.tile([P, H], F32, name="o_acc%d" % t, tag="o%d" % t)
                    o_acc.append(o_t)
            for t in range(NT):
                nc.tensor.matmul(
                    o_acc[t][:, jt * P:(jt + 1) * P], lhsT=prods[s][0][:, prods[s][1], t * P:(t + 1) * P], rhs=ident_f[:],
                    is_transpose=True, start=(s == 0), stop=(s == TILES - 1),
                )

        n_mx = 0
        n_gate = 0
        n_mult = 0
        n_nc = 0
        ready = 0
        step = 0
        c0_pass = 0
        while n_mult < TILES:
            if 5 <= step + AHEAD < n_units:
                load_unit(step + AHEAD)
            old_mx, old_gate = n_mx, n_gate
            if step in QFIRST:
                quantize_unit(step - 1)
            for name in hooks.get((step, 0), ()):
                tasks[name]()
            if step < LOOK_FROM:
                interleave_part(step, "g")
                interleave_part(step, "s")
            if step < n_units:
                interleave_part(step, "v")
            for name in hooks.get((step, 1), ()):
                tasks[name]()
            for r in range(HEAD_DUMMY.get(step, 0)):
                nc.tensor.matmul(scr[:], lhsT=ones_b[:], rhs=raws[step][:, 0, 0:H], start=True, stop=True)
            if 1 <= step <= n_units and step not in QFIRST:
                quantize_unit(step - 1)
            if LOOK_FROM <= step + 1 < n_units:
                interleave_part(step + 1, "g")
                interleave_part(step + 1, "s")
            if 1 <= step <= n_units:
                u = step - 1
                if u < n_chunk_units:
                    c, g0, ng = units[u]
                    if g0 == 4:
                        ready = JT * (c + 1)
                else:
                    ready += 1
            todo = list(range(n_gate, min(n_gate + 2, old_mx)))
            if todo:
                gate(todo)
                n_gate += len(todo)
            first_mult = n_mult
            todo = list(range(n_mult, min(n_mult + 2, old_gate, n_nc)))
            if todo:
                mult(todo)
                n_mult += len(todo)
            for name in hooks.get((step, 2), ()):
                tasks[name]()
            if step >= 5 and c0_pass < NG:
                if c0_pass == 0:
                    for jt in range(JT):
                        acc0 = psum.tile([P, NODES], F32, name="acc0", tag="o%d" % jt)
                        accs[jt] = acc0
                while c0_pass < min(NG, step):
                    for jt in range(JT):
                        mx_pass(jt, c0_pass)
                    c0_pass += 1
                if c0_pass == NG:
                    n_mx = JT
            for r in range(2):
                if JT <= n_mx < ready and n_gate >= n_mx - 2 and n_gate >= JT:
                    acc = psum.tile([P, NODES], F32, name="acc", tag=("a0", "a1", "t1")[n_mx % 3])
                    accs[n_mx] = acc
                    for g in range(NG):
                        mx_pass(n_mx, g)
                    n_mx += 1
            if BOUND_DUMMY and n_mx == old_mx and (n_gate == n_mx or n_mx == JT) and JT <= n_mx < TILES and step < n_units:
                scr2 = psum.tile([P, NODES], F32, name="scr2", tag="a%d" % (n_mx % 2))
                for r in range(BOUND_DUMMY):
                    nc.tensor.matmul(scr2[:], lhsT=ones_b[:], rhs=first_columns(step), start=True, stop=True)
            todo = list(range(n_nc, min(n_nc + 2, n_mx)))
            if todo and (len(nc_calls) < 1 or n_mult > nc_calls[-1]):
                turn_nc(todo)
                n_nc += len(todo)
            for s in range(first_mult, n_mult):
                add_up(s)
            step += 1

        o32s = []
        o8s = []
        for t in range(NT):
            o32 = out_pool.tile([P, H], F32, name="o32")
            o32s.append(o32)
            o8 = out_pool.tile([P, H], FP8, name="o8")
            o8s.append(o8)
        def put(eng, kind, t):
            rows = slice(t * P, (t + 1) * P)
            if kind == "f":
                if eng == "v":
                    nc.vector.tensor_copy(out=o32s[t][:], in_=o_acc[t][:])
                else:
                    nc.scalar.copy(out=o32s[t][:], in_=o_acc[t][:])
                nc.sync.dma_start(out=out_0[rows, :], in_=o32s[t][:])
            else:
                if eng == "v":
                    nc.vector.tensor_scalar(
                        out=o8s[t][:], in0=o_acc[t][:], scalar1=Y_SCALE, scalar2=None, op0=ALU.mult, saturate=False)
                else:
                    nc.scalar.activation(out=o8s[t][:], in_=o_acc[t][:], func=ACT.Copy, scale=Y_SCALE, saturate=False)
                nc.sync.dma_start(out=out_1[rows, :], in_=o8s[t][:].bitcast(U8))

        for i in range(max(len(OUT_V), len(OUT_S))):
            if i < len(OUT_S):
                put("s", OUT_S[i][0], OUT_S[i][1])
            if i < len(OUT_V):
                put("v", OUT_V[i][0], OUT_V[i][1])
